import numpy as np
import ml_dtypes


def mxq(x, axis, fmt="e4m3"):
    dtype, down = {"e4m3": (ml_dtypes.float8_e4m3fn, 7), "e5m2": (ml_dtypes.float8_e5m2, 14)}[fmt]
    v = np.moveaxis(np.asarray(x, np.float32).astype(ml_dtypes.bfloat16).astype(np.float64), axis, -1)
    blocks = v.reshape(v.shape[:-1] + (-1, 32))
    amax = np.abs(blocks).max(-1, keepdims=True)
    byte = np.maximum(np.where(amax > 0, np.frexp(amax)[1] - 1 + 127, 0) - down, 1)
    scale = np.exp2(byte - 127.0)
    codes = (blocks / scale).astype(np.float32).astype(dtype).astype(np.float64)
    return np.moveaxis((codes * scale).reshape(v.shape), -1, axis)


WIDE = False


def mx_kscale(k):
    if not WIDE:
        return np.ones(k)
    levels = np.array([10, -10, 5, -5, 0])
    a = np.random.permutation(np.resize(levels, k // 512 * 4)).reshape(k // 512, 4)
    idx = np.arange(k)
    return np.exp2(a[idx // 512, idx % 128 // 32])


BF16 = ml_dtypes.bfloat16


def bf(x):
    return np.asarray(x, np.float32).astype(BF16)


def f64(x):
    return np.asarray(x).astype(np.float64)


N, D, O, H, W = 8, 512, 128, 32, 32
K = D + D
P = H * W


def exp_softmax_pool(y):
    a = np.exp(y)
    e = np.exp(a - a.max(-1, keepdims=True))
    sm = e / e.sum(-1, keepdims=True)
    return (sm * y).sum(-1)


def setup_inputs():
    s = mx_kscale(K)
    return {"x1": bf(np.random.standard_normal((N, D, H, W)) * 0.5 * s[:D][None, :, None, None]),
            "x2": bf(np.random.standard_normal((N, D, H, W)) * 0.5 * s[D:][None, :, None, None]),
            "c1_w": bf(np.random.standard_normal((O, K)) / np.sqrt(K) / s), "c1_b": bf(np.random.standard_normal(O) * 0.3),
            "c2_w": bf(np.random.standard_normal((O, K)) / np.sqrt(K) / s), "c2_b": bf(np.random.standard_normal(O) * 0.3)}


def reference(x1, x2, c1_w, c1_b, c2_w, c2_b):
    xc = np.concatenate([f64(x1), f64(x2)], axis=1).reshape(N, K, P)
    xq = mxq(xc, 1, "e4m3")
    x1x = (mxq(f64(c1_w), 1, "e4m3") @ xq) + f64(c1_b)[None, :, None]
    x2x = (mxq(f64(c2_w), 1, "e4m3") @ xq) + f64(c2_b)[None, :, None]
    return exp_softmax_pool(x1x), exp_softmax_pool(x2x)

@@ -1,0 +1,244 @@
+from contextlib import ExitStack
+
+import concourse.mybir as mybir
+from concourse.masks import make_identity
+
+FP8X4 = mybir.dt.float8_e4m3fn_x4
+BF16 = mybir.dt.bfloat16
+F32 = mybir.dt.float32
+U32 = mybir.dt.uint32
+U8 = mybir.dt.uint8
+ACT = mybir.ActivationFunctionType
+ALU = mybir.AluOpType
+AX = mybir.AxisListType
+
+P = 128
+PACK = 4
+IMGS = 8
+TILES = 2 * IMGS
+POS = 1024
+HALF = 512
+RUN = 4
+RAW_BUFS = 8
+
+FLOPS = 2 * IMGS * 2 * P * 1024 * POS
+
+
+def split_of(k):
+    return (512, 512)
+
+
+def tile_fr_pa_t_kernel(tc, x1, x2, c1_w, c1_b, c2_w, c2_b, out_0, out_1):
+    nc = tc.nc
+    with ExitStack() as ctx:
+        ctx.enter_context(tc.manual_schedule())
+        const = ctx.enter_context(tc.tile_pool(name="const", bufs=1))
+        rawp = ctx.enter_context(tc.tile_pool(name="rawp", bufs=RAW_BUFS))
+        grpp = ctx.enter_context(tc.tile_pool(name="grpp", bufs=3))
+        codp = ctx.enter_context(tc.tile_pool(name="codp", bufs=4))
+        work = ctx.enter_context(tc.tile_pool(name="work", bufs=3))
+        small = ctx.enter_context(tc.tile_pool(name="small", bufs=4))
+        psum = ctx.enter_context(tc.psum_pool(name="psum", bufs=8))
+
+        ident = const.tile([P, P], F32, name="ident")
+        w_sb = const.tile([P, 2, 1024], BF16, name="w_sb")
+        b_rows = const.tile([P, P], BF16, name="b_rows")
+        b_f32 = const.tile([P, P], F32, name="b_f32")
+        bias = const.tile([P, 2], F32, name="bias")
+        res = const.tile([P, P], F32, name="res")
+        w_grp = const.tile([P, 2, 2 * P * PACK], BF16, name="w_grp", align_bytes=64)
+        w_cod = const.tile([P, 2 * 2 * P], U32, name="w_cod", align_bytes=64)
+        w_scl = const.tile([P, 2 * 2 * P], U8, name="w_scl", align_bytes=64)
+        sum_e = const.tile([P, 2 * IMGS], F32, name="sum_e")
+        sum_ey = const.tile([P, 2 * IMGS, 2], F32, name="sum_ey")
+        junk = const.tile([P, HALF], F32, name="junk")
+
+        raws = {}
+        grps = {}
+        cods = {}
+        ys = {}
+        acts = {}
+        peaks = {}
+        exps = {}
+
+        def load(k):
+            if k >= TILES:
+                return
+            src = (x1, x2)[k % 2][k // 2].rearrange("(p t) h w -> p t (h w)", t=PACK)
+            raw = rawp.tile([P, PACK, POS], BF16, name="raw")
+            raws[k] = raw
+            if k == 0:
+                for h in range(2):
+                    cols = slice(h * HALF, (h + 1) * HALF)
+                    nc.sync.dma_start(out=raw[:, :, cols], in_=src[:, :, cols])
+            else:
+                nc.sync.dma_start(out=raw[:], in_=src)
+
+        def views(k, lo, hi):
+            if k not in grps:
+                grp = grpp.tile([P, POS, PACK], BF16, name="grp", align_bytes=64)
+                grps[k] = grp
+            return (
+                grps[k][:, lo:hi, :].rearrange("p (c r) t -> p c t r", r=RUN),
+                raws[k][:, :, lo:hi].rearrange("p t (c r) -> p c t r", r=RUN),
+            )
+
+        def regroup_s(k):
+            if 0 <= k < TILES:
+                dst, src = views(k, split_of(k)[1], POS)
+                nc.scalar.copy(out=dst, in_=src)
+
+        def regroup_g(k):
+            if 0 <= k < TILES and split_of(k)[1] > split_of(k)[0]:
+                dst, src = views(k, split_of(k)[0], split_of(k)[1])
+                nc.gpsimd.tensor_scalar(out=dst, in0=src, scalar1=1.0, scalar2=0.0, op0=ALU.mult, op1=ALU.add)
+
+        def regroup_v(k):
+            if 0 <= k < TILES:
+                dst, src = views(k, 0, split_of(k)[0])
+                nc.vector.tensor_copy(out=dst, in_=src)
+                load(k + RAW_BUFS)
+
+        def quantise(k):
+            if 0 <= k < TILES:
+                cod = codp.tile([P, POS], U32, name="cod", align_bytes=64)
+                scl = codp.tile([P, POS], U8, name="scl", align_bytes=64)
+                cods[k] = (cod, scl)
+                nc.vector.quantize_mx(
+                    out=cod[:].bitcast(FP8X4), scales=scl[:], in_=grps[k][:].rearrange("p w t -> p (w t)")
+                )
+
+        def project(n):
+            if not 0 <= n < IMGS:
+                return
+            for i in range(2):
+                for h in range(2):
+                    y = psum.tile([P, HALF], F32, name="y", tag="bank")
+                    ys[(n, i, h)] = y
+                    for g in range(2):
+                        wc = slice((i * 2 + g) * P, (i * 2 + g + 1) * P)
+                        xc = slice(h * HALF, (h + 1) * HALF)
+                        cod, scl = cods[2 * n + g]
+                        nc.tensor.matmul_mx(
+                            out=y[:],
+                            lhsT=w_cod[:, wc].bitcast(FP8X4),
+                            lhsT_scale=w_scl[:, wc],
+                            rhs=cod[:, xc].bitcast(FP8X4),
+                            rhs_scale=scl[:, xc],
+                            start=(g == 0),
+                            stop=(g == 1),
+                        )
+
+        def exp_of_y(n):
+            if not 0 <= n < IMGS:
+                return
+            for i in range(2):
+                a = work.tile([P, POS], F32, name="a")
+                acts[(n, i)] = a
+                for h in range(2):
+                    nc.scalar.activation(
+                        out=a[:, h * HALF : (h + 1) * HALF], in_=ys[(n, i, h)][:], func=ACT.Exp,
+                        bias=bias[:, i : i + 1], scale=1.0,
+                    )
+
+        def peak(n):
+            if not 0 <= n < IMGS:
+                return
+            for i in range(2):
+                negmax = small.tile([P, 1], F32, name="negmax")
+                peaks[(n, i)] = negmax
+                nc.vector.tensor_reduce(out=negmax[:], in_=acts[(n, i)][:], axis=AX.X, op=ALU.max, negate=True)
+
+        def exp_of_a(n):
+            if not 0 <= n < IMGS:
+                return
+            for i in range(2):
+                e = work.tile([P, POS], F32, name="e")
+                exps[(n, i)] = e
+                unit = i * IMGS + n
+                nc.scalar.activation(
+                    out=e[:], in_=acts[(n, i)][:], func=ACT.Exp, bias=peaks[(n, i)][:], scale=1.0,
+                    accum_out=sum_e[:, unit : unit + 1],
+                )
+
+        def weigh(n):
+            if not 0 <= n < IMGS:
+                return
+            for i in range(2):
+                unit = i * IMGS + n
+                for h in range(2):
+                    nc.vector.scalar_tensor_tensor(
+                        out=junk[:], in0=ys[(n, i, h)][:], scalar=bias[:, i : i + 1],
+                        in1=exps[(n, i)][:, h * HALF : (h + 1) * HALF], op0=ALU.add, op1=ALU.mult,
+                        accum_out=sum_ey[:, unit, h : h + 1],
+                    )
+
+        def weight(i):
+            wt = psum.tile([P, 2, 2, P], F32, name="wt", tag="bank")
+            words = w_sb[:, i, :].bitcast(F32).rearrange("o (g p u) -> o g u p", g=2, u=2)
+            for g in range(2):
+                for u in range(2):
+                    nc.tensor.transpose(wt[:, g, u, :], words[:, g, u, :], ident[:])
+            nc.vector.tensor_copy(
+                out=w_grp[:, i, :].bitcast(F32).rearrange("p (g o u) -> p g o u", g=2, u=2),
+                in_=wt[:].rearrange("p g u o -> p g o u"),
+            )
+
+        def weight_quantise(i):
+            wc = slice(i * 2 * P, (i + 1) * 2 * P)
+            nc.vector.quantize_mx(out=w_cod[:, wc].bitcast(FP8X4), scales=w_scl[:, wc], in_=w_grp[:, i, :])
+
+        make_identity(nc, ident[:])
+        nc.vector.memset(b_rows[:], 0.0)
+        nc.vector.memset(res[:], 0.0)
+        load(0)
+        nc.sync.dma_start(out=w_sb[:, 0, :], in_=c1_w)
+        load(1)
+        nc.sync.dma_start(out=w_sb[:, 1, :], in_=c2_w)
+        nc.sync.dma_start(out=b_rows[0:1, :], in_=c1_b.unsqueeze(0))
+        nc.sync.dma_start(out=b_rows[1:2, :], in_=c2_b.unsqueeze(0))
+        for k in range(2, RAW_BUFS):
+            load(k)
+
+        regroup_s(0)
+        regroup_g(0)
+        regroup_v(0)
+        weight(0)
+        regroup_s(1)
+        regroup_g(1)
+        quantise(0)
+        regroup_v(1)
+        weight_quantise(0)
+        weight(1)
+        nc.vector.tensor_copy(out=b_f32[:], in_=b_rows[:])
+        bt = psum.tile([P, P], F32, name="bt", tag="bank")
+        nc.tensor.transpose(bt[:], b_f32[:], ident[:])
+        weight_quantise(1)
+        nc.vector.tensor_copy(out=bias[:], in_=bt[:, 0:2])
+
+        for n in range(-1, IMGS):
+            exp_of_y(n)
+            peak(n)
+            regroup_s(2 * n + 4)
+            regroup_g(2 * n + 4)
+            quantise(2 * n + 3)
+            project(n + 1)
+            regroup_v(2 * n + 4)
+            exp_of_a(n)
+            weigh(n)
+            regroup_s(2 * n + 5)
+            regroup_g(2 * n + 5)
+            quantise(2 * n + 4)
+            regroup_v(2 * n + 5)
+
+        num = const.tile([P, 2 * IMGS], F32, name="num")
+        nc.vector.tensor_tensor(out=num[:], in0=sum_ey[:, :, 0], in1=sum_ey[:, :, 1], op=ALU.add)
+        rec = const.tile([P, 2 * IMGS], F32, name="rec")
+        nc.vector.reciprocal(out=rec[:], in_=sum_e[:])
+        nc.vector.tensor_tensor(out=res[:, 0 : 2 * IMGS], in0=num[:], in1=rec[:], op=ALU.mult)
+        rt = psum.tile([P, P], F32, name="rt", tag="bank")
+        nc.tensor.transpose(rt[:], res[:], ident[:])
+        rows = const.tile([P, P], F32, name="rows")
+        nc.vector.tensor_copy(out=rows[:], in_=rt[:])
+        nc.sync.dma_start(out=out_0, in_=rows[0:IMGS, :])
+        nc.sync.dma_start(out=out_1, in_=rows[IMGS : 2 * IMGS, :])

@@ -51,7 +51,6 @@ def tile_fr_pa_t_kernel(tc, x1, x2, c1_w, c1_b, c2_w, c2_b, out_0, out_1):
         w_scl = const.tile([P, 2 * 2 * P], U8, name="w_scl", align_bytes=64)
         sum_e = const.tile([P, 2 * IMGS], F32, name="sum_e")
         sum_ey = const.tile([P, 2 * IMGS, 2], F32, name="sum_ey")
-        junk = const.tile([P, HALF], F32, name="junk")
 
         raws = {}
         grps = {}
@@ -168,7 +167,7 @@ def tile_fr_pa_t_kernel(tc, x1, x2, c1_w, c1_b, c2_w, c2_b, out_0, out_1):
                 unit = i * IMGS + n
                 for h in range(2):
                     nc.vector.scalar_tensor_tensor(
-                        out=junk[:], in0=ys[(n, i, h)][:], scalar=bias[:, i : i + 1],
+                        out=exps[(n, i)][:, h * HALF : (h + 1) * HALF], in0=ys[(n, i, h)][:], scalar=bias[:, i : i + 1],
                         in1=exps[(n, i)][:, h * HALF : (h + 1) * HALF], op0=ALU.add, op1=ALU.mult,
                         accum_out=sum_ey[:, unit, h : h + 1],
                     )

@@ -25,7 +25,7 @@ FLOPS = 2 * IMGS * 2 * P * 1024 * POS
 
 
 def split_of(k):
-    return (512, 512)
+    return (512, 512) if k < 4 else (288, 608)
 
 
 def tile_fr_pa_t_kernel(tc, x1, x2, c1_w, c1_b, c2_w, c2_b, out_0, out_1):
@@ -89,8 +89,12 @@ def tile_fr_pa_t_kernel(tc, x1, x2, c1_w, c1_b, c2_w, c2_b, out_0, out_1):
 
         def regroup_g(k):
             if 0 <= k < TILES and split_of(k)[1] > split_of(k)[0]:
-                dst, src = views(k, split_of(k)[0], split_of(k)[1])
-                nc.gpsimd.tensor_scalar(out=dst, in0=src, scalar1=1.0, scalar2=0.0, op0=ALU.mult, op1=ALU.add)
+                lo, hi = split_of(k)
+                views(k, lo, hi)
+                nc.gpsimd.tensor_scalar(
+                    out=grps[k][:, lo:hi, :], in0=raws[k][:, :, lo:hi].rearrange("p t w -> p w t"),
+                    scalar1=1.0, scalar2=0.0, op0=ALU.mult, op1=ALU.add,
+                )
 
         def regroup_v(k):
             if 0 <= k < TILES:

@@ -31,7 +31,7 @@ def split_of(k):
 def tile_fr_pa_t_kernel(tc, x1, x2, c1_w, c1_b, c2_w, c2_b, out_0, out_1):
     nc = tc.nc
     with ExitStack() as ctx:
-        ctx.enter_context(tc.manual_schedule())
+        pass
         const = ctx.enter_context(tc.tile_pool(name="const", bufs=1))
         rawp = ctx.enter_context(tc.tile_pool(name="rawp", bufs=RAW_BUFS))
         grpp = ctx.enter_context(tc.tile_pool(name="grpp", bufs=3))

@@ -20,21 +20,26 @@ POS = 1024
 HALF = 512
 RUN = 4
 RAW_BUFS = 8
+HEAD_SPLITS = ((544, 544), (448, 448), (576, 576), (576, 576))
+EVEN_SPLIT = (272, 624)
+ODD_SPLIT = (208, 608)
 
 FLOPS = 2 * IMGS * 2 * P * 1024 * POS
 
 
 def split_of(k):
-    return (512, 512) if k < 4 else (288, 608)
+    if k < len(HEAD_SPLITS):
+        return HEAD_SPLITS[k]
+    return EVEN_SPLIT if k % 2 == 0 else ODD_SPLIT
 
 
 def tile_fr_pa_t_kernel(tc, x1, x2, c1_w, c1_b, c2_w, c2_b, out_0, out_1):
     nc = tc.nc
     with ExitStack() as ctx:
-        pass
+        ctx.enter_context(tc.manual_schedule())
         const = ctx.enter_context(tc.tile_pool(name="const", bufs=1))
         rawp = ctx.enter_context(tc.tile_pool(name="rawp", bufs=RAW_BUFS))
-        grpp = ctx.enter_context(tc.tile_pool(name="grpp", bufs=3))
+        grpp = ctx.enter_context(tc.tile_pool(name="grpp", bufs=2))
         codp = ctx.enter_context(tc.tile_pool(name="codp", bufs=4))
         work = ctx.enter_context(tc.tile_pool(name="work", bufs=3))
         small = ctx.enter_context(tc.tile_pool(name="small", bufs=4))
@@ -46,11 +51,15 @@ def tile_fr_pa_t_kernel(tc, x1, x2, c1_w, c1_b, c2_w, c2_b, out_0, out_1):
         b_f32 = const.tile([P, P], F32, name="b_f32")
         bias = const.tile([P, 2], F32, name="bias")
         res = const.tile([P, P], F32, name="res")
+        warm = const.tile([P, 1], F32, name="warm")
         w_grp = const.tile([P, 2, 2 * P * PACK], BF16, name="w_grp", align_bytes=64)
         w_cod = const.tile([P, 2 * 2 * P], U32, name="w_cod", align_bytes=64)
         w_scl = const.tile([P, 2 * 2 * P], U8, name="w_scl", align_bytes=64)
         sum_e = const.tile([P, 2 * IMGS], F32, name="sum_e")
         sum_ey = const.tile([P, 2 * IMGS, 2], F32, name="sum_ey")
+        num = const.tile([P, 2 * IMGS], F32, name="num")
+        rec = const.tile([P, 2 * IMGS], F32, name="rec")
+        rows = const.tile([P, P], F32, name="rows")
 
         raws = {}
         grps = {}
@@ -67,9 +76,9 @@ def tile_fr_pa_t_kernel(tc, x1, x2, c1_w, c1_b, c2_w, c2_b, out_0, out_1):
             raw = rawp.tile([P, PACK, POS], BF16, name="raw")
             raws[k] = raw
             if k == 0:
-                for h in range(2):
-                    cols = slice(h * HALF, (h + 1) * HALF)
-                    nc.sync.dma_start(out=raw[:, :, cols], in_=src[:, :, cols])
+                cut = split_of(0)[0]
+                nc.sync.dma_start(out=raw[:, :, 0:cut], in_=src[:, :, 0:cut])
+                nc.sync.dma_start(out=raw[:, :, cut:POS], in_=src[:, :, cut:POS])
             else:
                 nc.sync.dma_start(out=raw[:], in_=src)
 
@@ -83,37 +92,31 @@ def tile_fr_pa_t_kernel(tc, x1, x2, c1_w, c1_b, c2_w, c2_b, out_0, out_1):
             )
 
         def regroup_s(k):
-            if 0 <= k < TILES:
-                dst, src = views(k, split_of(k)[1], POS)
-                nc.scalar.copy(out=dst, in_=src)
+            dst, src = views(k, split_of(k)[1], POS)
+            nc.scalar.copy(out=dst, in_=src)
 
         def regroup_g(k):
-            if 0 <= k < TILES and split_of(k)[1] > split_of(k)[0]:
-                lo, hi = split_of(k)
-                views(k, lo, hi)
+            lo, hi = split_of(k)
+            if hi > lo:
                 nc.gpsimd.tensor_scalar(
                     out=grps[k][:, lo:hi, :], in0=raws[k][:, :, lo:hi].rearrange("p t w -> p w t"),
                     scalar1=1.0, scalar2=0.0, op0=ALU.mult, op1=ALU.add,
                 )
 
         def regroup_v(k):
-            if 0 <= k < TILES:
-                dst, src = views(k, 0, split_of(k)[0])
-                nc.vector.tensor_copy(out=dst, in_=src)
-                load(k + RAW_BUFS)
+            dst, src = views(k, 0, split_of(k)[0])
+            nc.vector.tensor_copy(out=dst, in_=src)
+            load(k + RAW_BUFS)
 
         def quantise(k):
-            if 0 <= k < TILES:
-                cod = codp.tile([P, POS], U32, name="cod", align_bytes=64)
-                scl = codp.tile([P, POS], U8, name="scl", align_bytes=64)
-                cods[k] = (cod, scl)
-                nc.vector.quantize_mx(
-                    out=cod[:].bitcast(FP8X4), scales=scl[:], in_=grps[k][:].rearrange("p w t -> p (w t)")
-                )
+            cod = codp.tile([P, POS], U32, name="cod", align_bytes=64)
+            scl = codp.tile([P, POS], U8, name="scl", align_bytes=64)
+            cods[k] = (cod, scl)
+            nc.vector.quantize_mx(
+                out=cod[:].bitcast(FP8X4), scales=scl[:], in_=grps[k][:].rearrange("p w t -> p (w t)")
+            )
 
         def project(n):
-            if not 0 <= n < IMGS:
-                return
             for i in range(2):
                 for h in range(2):
                     y = psum.tile([P, HALF], F32, name="y", tag="bank")
@@ -133,8 +136,6 @@ def tile_fr_pa_t_kernel(tc, x1, x2, c1_w, c1_b, c2_w, c2_b, out_0, out_1):
                         )
 
         def exp_of_y(n):
-            if not 0 <= n < IMGS:
-                return
             for i in range(2):
                 a = work.tile([P, POS], F32, name="a")
                 acts[(n, i)] = a
@@ -145,16 +146,12 @@ def tile_fr_pa_t_kernel(tc, x1, x2, c1_w, c1_b, c2_w, c2_b, out_0, out_1):
                     )
 
         def peak(n):
-            if not 0 <= n < IMGS:
-                return
             for i in range(2):
                 negmax = small.tile([P, 1], F32, name="negmax")
                 peaks[(n, i)] = negmax
                 nc.vector.tensor_reduce(out=negmax[:], in_=acts[(n, i)][:], axis=AX.X, op=ALU.max, negate=True)
 
         def exp_of_a(n):
-            if not 0 <= n < IMGS:
-                return
             for i in range(2):
                 e = work.tile([P, POS], F32, name="e")
                 exps[(n, i)] = e
@@ -165,15 +162,15 @@ def tile_fr_pa_t_kernel(tc, x1, x2, c1_w, c1_b, c2_w, c2_b, out_0, out_1):
                 )
 
         def weigh(n):
-            if not 0 <= n < IMGS:
-                return
             for i in range(2):
                 unit = i * IMGS + n
+                if n == IMGS - 1 and i == 1:
+                    nc.vector.reciprocal(out=rec[:], in_=sum_e[:])
                 for h in range(2):
+                    half = exps[(n, i)][:, h * HALF : (h + 1) * HALF]
                     nc.vector.scalar_tensor_tensor(
-                        out=exps[(n, i)][:, h * HALF : (h + 1) * HALF], in0=ys[(n, i, h)][:], scalar=bias[:, i : i + 1],
-                        in1=exps[(n, i)][:, h * HALF : (h + 1) * HALF], op0=ALU.add, op1=ALU.mult,
-                        accum_out=sum_ey[:, unit, h : h + 1],
+                        out=half, in0=ys[(n, i, h)][:], scalar=bias[:, i : i + 1], in1=half,
+                        op0=ALU.add, op1=ALU.mult, accum_out=sum_ey[:, unit, h : h + 1],
                     )
 
         def weight(i):
@@ -191,7 +188,27 @@ def tile_fr_pa_t_kernel(tc, x1, x2, c1_w, c1_b, c2_w, c2_b, out_0, out_1):
             wc = slice(i * 2 * P, (i + 1) * 2 * P)
             nc.vector.quantize_mx(out=w_cod[:, wc].bitcast(FP8X4), scales=w_scl[:, wc], in_=w_grp[:, i, :])
 
+        def fill_s(k):
+            if k < TILES:
+                regroup_s(k)
+                regroup_g(k)
+
+        def fill_v(k):
+            if k == TILES - 2:
+                regroup_v(k + 1)
+                quantise(k)
+                quantise(k + 1)
+                project(IMGS - 1)
+            elif k < TILES - 2:
+                quantise(k)
+                if k + 1 < TILES:
+                    regroup_v(k + 1)
+                if k % 2 == 1:
+                    project(k // 2)
+
         make_identity(nc, ident[:])
+        nc.vector.memset(warm[:], 0.0)
+        nc.scalar.activation(out=warm[:], in_=warm[:], func=ACT.Exp)
         nc.vector.memset(b_rows[:], 0.0)
         nc.vector.memset(res[:], 0.0)
         load(0)
@@ -203,14 +220,11 @@ def tile_fr_pa_t_kernel(tc, x1, x2, c1_w, c1_b, c2_w, c2_b, out_0, out_1):
         for k in range(2, RAW_BUFS):
             load(k)
 
-        regroup_s(0)
-        regroup_g(0)
+        fill_s(0)
         regroup_v(0)
         weight(0)
-        regroup_s(1)
-        regroup_g(1)
-        quantise(0)
-        regroup_v(1)
+        fill_s(1)
+        fill_v(0)
         weight_quantise(0)
         weight(1)
         nc.vector.tensor_copy(out=b_f32[:], in_=b_rows[:])
@@ -218,30 +232,26 @@ def tile_fr_pa_t_kernel(tc, x1, x2, c1_w, c1_b, c2_w, c2_b, out_0, out_1):
         nc.tensor.transpose(bt[:], b_f32[:], ident[:])
         weight_quantise(1)
         nc.vector.tensor_copy(out=bias[:], in_=bt[:, 0:2])
+        fill_s(2)
+        fill_v(1)
+        fill_s(3)
+        fill_v(2)
 
-        for n in range(-1, IMGS):
+        for n in range(IMGS):
             exp_of_y(n)
             peak(n)
-            regroup_s(2 * n + 4)
-            regroup_g(2 * n + 4)
-            quantise(2 * n + 3)
-            project(n + 1)
-            regroup_v(2 * n + 4)
+            fill_s(2 * n + 4)
+            fill_v(2 * n + 3)
             exp_of_a(n)
             weigh(n)
-            regroup_s(2 * n + 5)
-            regroup_g(2 * n + 5)
-            quantise(2 * n + 4)
-            regroup_v(2 * n + 5)
+            fill_s(2 * n + 5)
+            fill_v(2 * n + 4)
 
-        num = const.tile([P, 2 * IMGS], F32, name="num")
+
         nc.vector.tensor_tensor(out=num[:], in0=sum_ey[:, :, 0], in1=sum_ey[:, :, 1], op=ALU.add)
-        rec = const.tile([P, 2 * IMGS], F32, name="rec")
-        nc.vector.reciprocal(out=rec[:], in_=sum_e[:])
         nc.vector.tensor_tensor(out=res[:, 0 : 2 * IMGS], in0=num[:], in1=rec[:], op=ALU.mult)
         rt = psum.tile([P, P], F32, name="rt", tag="bank")
         nc.tensor.transpose(rt[:], res[:], ident[:])
-        rows = const.tile([P, P], F32, name="rows")
         nc.vector.tensor_copy(out=rows[:], in_=rt[:])
         nc.sync.dma_start(out=out_0, in_=rows[0:IMGS, :])
         nc.sync.dma_start(out=out_1, in_=rows[IMGS : 2 * IMGS, :])

@@ -16,13 +16,14 @@ P = 128
 PACK = 4
 IMGS = 8
 TILES = 2 * IMGS
+UNITS = 2 * IMGS
 POS = 1024
 HALF = 512
 RUN = 4
 RAW_BUFS = 8
 HEAD_SPLITS = ((544, 544), (448, 448), (576, 576), (576, 576))
-EVEN_SPLIT = (272, 624)
-ODD_SPLIT = (208, 608)
+PE_POS = 256
+STEADY_SPLIT = (PE_POS, 768)
 
 FLOPS = 2 * IMGS * 2 * P * 1024 * POS
 
@@ -30,7 +31,7 @@ FLOPS = 2 * IMGS * 2 * P * 1024 * POS
 def split_of(k):
     if k < len(HEAD_SPLITS):
         return HEAD_SPLITS[k]
-    return EVEN_SPLIT if k % 2 == 0 else ODD_SPLIT
+    return STEADY_SPLIT
 
 
 def tile_fr_pa_t_kernel(tc, x1, x2, c1_w, c1_b, c2_w, c2_b, out_0, out_1):
@@ -43,9 +44,11 @@ def tile_fr_pa_t_kernel(tc, x1, x2, c1_w, c1_b, c2_w, c2_b, out_0, out_1):
         codp = ctx.enter_context(tc.tile_pool(name="codp", bufs=4))
         work = ctx.enter_context(tc.tile_pool(name="work", bufs=3))
         small = ctx.enter_context(tc.tile_pool(name="small", bufs=4))
-        psum = ctx.enter_context(tc.psum_pool(name="psum", bufs=8))
+        psum = ctx.enter_context(tc.psum_pool(name="psum", bufs=6))
+        psaux = ctx.enter_context(tc.psum_pool(name="psaux", bufs=2))
 
         ident = const.tile([P, P], F32, name="ident")
+        ident_b = const.tile([P, P], BF16, name="ident_b")
         w_sb = const.tile([P, 2, 1024], BF16, name="w_sb")
         b_rows = const.tile([P, P], BF16, name="b_rows")
         b_f32 = const.tile([P, P], F32, name="b_f32")
@@ -55,10 +58,10 @@ def tile_fr_pa_t_kernel(tc, x1, x2, c1_w, c1_b, c2_w, c2_b, out_0, out_1):
         w_grp = const.tile([P, 2, 2 * P * PACK], BF16, name="w_grp", align_bytes=64)
         w_cod = const.tile([P, 2 * 2 * P], U32, name="w_cod", align_bytes=64)
         w_scl = const.tile([P, 2 * 2 * P], U8, name="w_scl", align_bytes=64)
-        sum_e = const.tile([P, 2 * IMGS], F32, name="sum_e")
-        sum_ey = const.tile([P, 2 * IMGS, 2], F32, name="sum_ey")
-        num = const.tile([P, 2 * IMGS], F32, name="num")
-        rec = const.tile([P, 2 * IMGS], F32, name="rec")
+        sum_e = const.tile([P, UNITS], F32, name="sum_e")
+        sum_ey = const.tile([P, UNITS, 2], F32, name="sum_ey")
+        num = const.tile([P, UNITS], F32, name="num")
+        rec = const.tile([P, UNITS], F32, name="rec")
         rows = const.tile([P, P], F32, name="rows")
 
         raws = {}
@@ -68,9 +71,13 @@ def tile_fr_pa_t_kernel(tc, x1, x2, c1_w, c1_b, c2_w, c2_b, out_0, out_1):
         acts = {}
         peaks = {}
         exps = {}
+        banks = {}
+
+        def column_of(u):
+            return (u % 2) * IMGS + u // 2
 
         def load(k):
-            if k >= TILES:
+            if not 0 <= k < TILES:
                 return
             src = (x1, x2)[k % 2][k // 2].rearrange("(p t) h w -> p t (h w)", t=PACK)
             raw = rawp.tile([P, PACK, POS], BF16, name="raw")
@@ -82,33 +89,56 @@ def tile_fr_pa_t_kernel(tc, x1, x2, c1_w, c1_b, c2_w, c2_b, out_0, out_1):
             else:
                 nc.sync.dma_start(out=raw[:], in_=src)
 
+        def through_pe(k):
+            return k >= len(HEAD_SPLITS)
+
         def views(k, lo, hi):
-            if k not in grps:
-                grp = grpp.tile([P, POS, PACK], BF16, name="grp", align_bytes=64)
-                grps[k] = grp
             return (
                 grps[k][:, lo:hi, :].rearrange("p (c r) t -> p c t r", r=RUN),
                 raws[k][:, :, lo:hi].rearrange("p t (c r) -> p c t r", r=RUN),
             )
 
-        def regroup_s(k):
-            dst, src = views(k, split_of(k)[1], POS)
-            nc.scalar.copy(out=dst, in_=src)
-
-        def regroup_g(k):
-            lo, hi = split_of(k)
-            if hi > lo:
-                nc.gpsimd.tensor_scalar(
-                    out=grps[k][:, lo:hi, :], in0=raws[k][:, :, lo:hi].rearrange("p t w -> p w t"),
-                    scalar1=1.0, scalar2=0.0, op0=ALU.mult, op1=ALU.add,
+        def spread(k):
+            if not 0 <= k < TILES or not through_pe(k):
+                return
+            bank = psaux.tile([P, PE_POS, PACK], BF16, name="bank", tag="aux")
+            banks[k] = bank
+            for c in range(PE_POS // P):
+                w = slice(c * P, (c + 1) * P)
+                nc.tensor.matmul(
+                    out=bank[:, w, :], lhsT=ident_b[:], rhs=raws[k][:, :, w].rearrange("p t w -> p w t"),
+                    start=True, stop=True,
                 )
 
+        def regroup_sg(k):
+            if not 0 <= k < TILES:
+                return
+            grp = grpp.tile([P, POS, PACK], BF16, name="grp", align_bytes=64)
+            grps[k] = grp
+            lo, hi = split_of(k)
+            dst, src = views(k, hi, POS)
+            nc.scalar.copy(out=dst, in_=src)
+            if hi > lo:
+                nc.gpsimd.tensor_scalar(
+                    out=grp[:, lo:hi, :], in0=raws[k][:, :, lo:hi].rearrange("p t w -> p w t"),
+                    scalar1=1.0, scalar2=0.0, op0=ALU.mult, op1=ALU.add,
+                )
+            if through_pe(k) and k % 2 == 0:
+                nc.scalar.copy(out=grp[:, 0:PE_POS, :], in_=banks[k][:])
+
         def regroup_v(k):
-            dst, src = views(k, 0, split_of(k)[0])
-            nc.vector.tensor_copy(out=dst, in_=src)
+            if not 0 <= k < TILES:
+                return
+            if not through_pe(k):
+                dst, src = views(k, 0, split_of(k)[0])
+                nc.vector.tensor_copy(out=dst, in_=src)
+            elif k % 2 == 1:
+                nc.vector.tensor_copy(out=grps[k][:, 0:PE_POS, :], in_=banks[k][:])
             load(k + RAW_BUFS)
 
         def quantise(k):
+            if not 0 <= k < TILES:
+                return
             cod = codp.tile([P, POS], U32, name="cod", align_bytes=64)
             scl = codp.tile([P, POS], U8, name="scl", align_bytes=64)
             cods[k] = (cod, scl)
@@ -116,65 +146,71 @@ def tile_fr_pa_t_kernel(tc, x1, x2, c1_w, c1_b, c2_w, c2_b, out_0, out_1):
                 out=cod[:].bitcast(FP8X4), scales=scl[:], in_=grps[k][:].rearrange("p w t -> p (w t)")
             )
 
-        def project(n):
-            for i in range(2):
-                for h in range(2):
-                    y = psum.tile([P, HALF], F32, name="y", tag="bank")
-                    ys[(n, i, h)] = y
-                    for g in range(2):
-                        wc = slice((i * 2 + g) * P, (i * 2 + g + 1) * P)
-                        xc = slice(h * HALF, (h + 1) * HALF)
-                        cod, scl = cods[2 * n + g]
-                        nc.tensor.matmul_mx(
-                            out=y[:],
-                            lhsT=w_cod[:, wc].bitcast(FP8X4),
-                            lhsT_scale=w_scl[:, wc],
-                            rhs=cod[:, xc].bitcast(FP8X4),
-                            rhs_scale=scl[:, xc],
-                            start=(g == 0),
-                            stop=(g == 1),
-                        )
-
-        def exp_of_y(n):
-            for i in range(2):
-                a = work.tile([P, POS], F32, name="a")
-                acts[(n, i)] = a
-                for h in range(2):
-                    nc.scalar.activation(
-                        out=a[:, h * HALF : (h + 1) * HALF], in_=ys[(n, i, h)][:], func=ACT.Exp,
-                        bias=bias[:, i : i + 1], scale=1.0,
+        def project(u):
+            if not 0 <= u < UNITS:
+                return
+            n, i = u // 2, u % 2
+            for h in range(2):
+                y = psum.tile([P, HALF], F32, name="y", tag="bank")
+                ys[(u, h)] = y
+                for g in range(2):
+                    wc = slice((i * 2 + g) * P, (i * 2 + g + 1) * P)
+                    xc = slice(h * HALF, (h + 1) * HALF)
+                    cod, scl = cods[2 * n + g]
+                    nc.tensor.matmul_mx(
+                        out=y[:],
+                        lhsT=w_cod[:, wc].bitcast(FP8X4),
+                        lhsT_scale=w_scl[:, wc],
+                        rhs=cod[:, xc].bitcast(FP8X4),
+                        rhs_scale=scl[:, xc],
+                        start=(g == 0),
+                        stop=(g == 1),
                     )
 
-        def peak(n):
-            for i in range(2):
-                negmax = small.tile([P, 1], F32, name="negmax")
-                peaks[(n, i)] = negmax
-                nc.vector.tensor_reduce(out=negmax[:], in_=acts[(n, i)][:], axis=AX.X, op=ALU.max, negate=True)
-
-        def exp_of_a(n):
-            for i in range(2):
-                e = work.tile([P, POS], F32, name="e")
-                exps[(n, i)] = e
-                unit = i * IMGS + n
+        def exp_of_y(u):
+            if not 0 <= u < UNITS:
+                return
+            a = work.tile([P, POS], F32, name="a")
+            acts[u] = a
+            for h in range(2):
                 nc.scalar.activation(
-                    out=e[:], in_=acts[(n, i)][:], func=ACT.Exp, bias=peaks[(n, i)][:], scale=1.0,
-                    accum_out=sum_e[:, unit : unit + 1],
+                    out=a[:, h * HALF : (h + 1) * HALF], in_=ys[(u, h)][:], func=ACT.Exp,
+                    bias=bias[:, u % 2 : u % 2 + 1], scale=1.0,
                 )
 
-        def weigh(n):
-            for i in range(2):
-                unit = i * IMGS + n
-                if n == IMGS - 1 and i == 1:
-                    nc.vector.reciprocal(out=rec[:], in_=sum_e[:])
-                for h in range(2):
-                    half = exps[(n, i)][:, h * HALF : (h + 1) * HALF]
-                    nc.vector.scalar_tensor_tensor(
-                        out=half, in0=ys[(n, i, h)][:], scalar=bias[:, i : i + 1], in1=half,
-                        op0=ALU.add, op1=ALU.mult, accum_out=sum_ey[:, unit, h : h + 1],
-                    )
+        def peak(u):
+            if not 0 <= u < UNITS:
+                return
+            negmax = small.tile([P, 1], F32, name="negmax")
+            peaks[u] = negmax
+            nc.vector.tensor_reduce(out=negmax[:], in_=acts[u][:], axis=AX.X, op=ALU.max, negate=True)
+
+        def exp_of_a(u):
+            if not 0 <= u < UNITS:
+                return
+            e = work.tile([P, POS], F32, name="e")
+            exps[u] = e
+            col = column_of(u)
+            nc.scalar.activation(
+                out=e[:], in_=acts[u][:], func=ACT.Exp, bias=peaks[u][:], scale=1.0,
+                accum_out=sum_e[:, col : col + 1],
+            )
+
+        def weigh(u):
+            if not 0 <= u < UNITS:
+                return
+            col = column_of(u)
+            if u == UNITS - 1:
+                nc.vector.reciprocal(out=rec[:], in_=sum_e[:])
+            for h in range(2):
+                half = exps[u][:, h * HALF : (h + 1) * HALF]
+                nc.vector.scalar_tensor_tensor(
+                    out=half, in0=ys[(u, h)][:], scalar=bias[:, u % 2 : u % 2 + 1], in1=half,
+                    op0=ALU.add, op1=ALU.mult, accum_out=sum_ey[:, col, h : h + 1],
+                )
 
         def weight(i):
-            wt = psum.tile([P, 2, 2, P], F32, name="wt", tag="bank")
+            wt = psaux.tile([P, 2, 2, P], F32, name="wt", tag="aux")
             words = w_sb[:, i, :].bitcast(F32).rearrange("o (g p u) -> o g u p", g=2, u=2)
             for g in range(2):
                 for u in range(2):
@@ -188,25 +224,20 @@ def tile_fr_pa_t_kernel(tc, x1, x2, c1_w, c1_b, c2_w, c2_b, out_0, out_1):
             wc = slice(i * 2 * P, (i + 1) * 2 * P)
             nc.vector.quantize_mx(out=w_cod[:, wc].bitcast(FP8X4), scales=w_scl[:, wc], in_=w_grp[:, i, :])
 
-        def fill_s(k):
-            if k < TILES:
-                regroup_s(k)
-                regroup_g(k)
+        def weights_first():
+            weight(0)
 
-        def fill_v(k):
-            if k == TILES - 2:
-                regroup_v(k + 1)
-                quantise(k)
-                quantise(k + 1)
-                project(IMGS - 1)
-            elif k < TILES - 2:
-                quantise(k)
-                if k + 1 < TILES:
-                    regroup_v(k + 1)
-                if k % 2 == 1:
-                    project(k // 2)
+        def weights_rest():
+            weight_quantise(0)
+            weight(1)
+            nc.vector.tensor_copy(out=b_f32[:], in_=b_rows[:])
+            bt = psaux.tile([P, P], F32, name="bt", tag="aux")
+            nc.tensor.transpose(bt[:], b_f32[:], ident[:])
+            weight_quantise(1)
+            nc.vector.tensor_copy(out=bias[:], in_=bt[:, 0:2])
 
         make_identity(nc, ident[:])
+        make_identity(nc, ident_b[:])
         nc.vector.memset(warm[:], 0.0)
         nc.scalar.activation(out=warm[:], in_=warm[:], func=ACT.Exp)
         nc.vector.memset(b_rows[:], 0.0)
@@ -220,37 +251,24 @@ def tile_fr_pa_t_kernel(tc, x1, x2, c1_w, c1_b, c2_w, c2_b, out_0, out_1):
         for k in range(2, RAW_BUFS):
             load(k)
 
-        fill_s(0)
-        regroup_v(0)
-        weight(0)
-        fill_s(1)
-        fill_v(0)
-        weight_quantise(0)
-        weight(1)
-        nc.vector.tensor_copy(out=b_f32[:], in_=b_rows[:])
-        bt = psum.tile([P, P], F32, name="bt", tag="bank")
-        nc.tensor.transpose(bt[:], b_f32[:], ident[:])
-        weight_quantise(1)
-        nc.vector.tensor_copy(out=bias[:], in_=bt[:, 0:2])
-        fill_s(2)
-        fill_v(1)
-        fill_s(3)
-        fill_v(2)
-
-        for n in range(IMGS):
-            exp_of_y(n)
-            peak(n)
-            fill_s(2 * n + 4)
-            fill_v(2 * n + 3)
-            exp_of_a(n)
-            weigh(n)
-            fill_s(2 * n + 5)
-            fill_v(2 * n + 4)
-
+        for u in range(-4, UNITS):
+            spread(u + 4)
+            exp_of_y(u + 1)
+            quantise(u + 3)
+            project(u + 2)
+            exp_of_a(u)
+            regroup_sg(u + 4)
+            regroup_v(u + 4)
+            if u == -4:
+                weights_first()
+            if u == -3:
+                weights_rest()
+            peak(u + 1)
+            weigh(u)
 
         nc.vector.tensor_tensor(out=num[:], in0=sum_ey[:, :, 0], in1=sum_ey[:, :, 1], op=ALU.add)
-        nc.vector.tensor_tensor(out=res[:, 0 : 2 * IMGS], in0=num[:], in1=rec[:], op=ALU.mult)
-        rt = psum.tile([P, P], F32, name="rt", tag="bank")
+        nc.vector.tensor_tensor(out=res[:, 0:UNITS], in0=num[:], in1=rec[:], op=ALU.mult)
+        rt = psaux.tile([P, P], F32, name="rt", tag="aux")
         nc.tensor.transpose(rt[:], res[:], ident[:])
         nc.vector.tensor_copy(out=rows[:], in_=rt[:])
         nc.sync.dma_start(out=out_0, in_=rows[0:IMGS, :])

@@ -23,15 +23,16 @@ RUN = 4
 RAW_BUFS = 8
 HEAD_SPLITS = ((544, 544), (448, 448), (576, 576), (576, 576))
 PE_POS = 256
-STEADY_SPLIT = (PE_POS, 768)
+V_POS = 128
+G_POS = 384
 
 FLOPS = 2 * IMGS * 2 * P * 1024 * POS
 
 
 def split_of(k):
     if k < len(HEAD_SPLITS):
-        return HEAD_SPLITS[k]
-    return STEADY_SPLIT
+        return (0,) + HEAD_SPLITS[k]
+    return (PE_POS, PE_POS + V_POS, PE_POS + V_POS + G_POS)
 
 
 def tile_fr_pa_t_kernel(tc, x1, x2, c1_w, c1_b, c2_w, c2_b, out_0, out_1):
@@ -83,7 +84,7 @@ def tile_fr_pa_t_kernel(tc, x1, x2, c1_w, c1_b, c2_w, c2_b, out_0, out_1):
             raw = rawp.tile([P, PACK, POS], BF16, name="raw")
             raws[k] = raw
             if k == 0:
-                cut = split_of(0)[0]
+                cut = split_of(0)[1]
                 nc.sync.dma_start(out=raw[:, :, 0:cut], in_=src[:, :, 0:cut])
                 nc.sync.dma_start(out=raw[:, :, cut:POS], in_=src[:, :, cut:POS])
             else:
@@ -115,7 +116,7 @@ def tile_fr_pa_t_kernel(tc, x1, x2, c1_w, c1_b, c2_w, c2_b, out_0, out_1):
                 return
             grp = grpp.tile([P, POS, PACK], BF16, name="grp", align_bytes=64)
             grps[k] = grp
-            lo, hi = split_of(k)
+            first, lo, hi = split_of(k)
             dst, src = views(k, hi, POS)
             nc.scalar.copy(out=dst, in_=src)
             if hi > lo:
@@ -123,17 +124,15 @@ def tile_fr_pa_t_kernel(tc, x1, x2, c1_w, c1_b, c2_w, c2_b, out_0, out_1):
                     out=grp[:, lo:hi, :], in0=raws[k][:, :, lo:hi].rearrange("p t w -> p w t"),
                     scalar1=1.0, scalar2=0.0, op0=ALU.mult, op1=ALU.add,
                 )
-            if through_pe(k) and k % 2 == 0:
+            if through_pe(k):
                 nc.scalar.copy(out=grp[:, 0:PE_POS, :], in_=banks[k][:])
 
         def regroup_v(k):
             if not 0 <= k < TILES:
                 return
-            if not through_pe(k):
-                dst, src = views(k, 0, split_of(k)[0])
-                nc.vector.tensor_copy(out=dst, in_=src)
-            elif k % 2 == 1:
-                nc.vector.tensor_copy(out=grps[k][:, 0:PE_POS, :], in_=banks[k][:])
+            first, lo, hi = split_of(k)
+            dst, src = views(k, first, lo)
+            nc.vector.tensor_copy(out=dst, in_=src)
             load(k + RAW_BUFS)
 
         def quantise(k):
@@ -252,7 +251,7 @@ def tile_fr_pa_t_kernel(tc, x1, x2, c1_w, c1_b, c2_w, c2_b, out_0, out_1):
             load(k)
 
         for u in range(-4, UNITS):
-            spread(u + 4)
+            spread(u + 5)
             exp_of_y(u + 1)
             quantise(u + 3)
             project(u + 2)

@@ -21,10 +21,10 @@ POS = 1024
 HALF = 512
 RUN = 4
 RAW_BUFS = 8
-HEAD_SPLITS = ((544, 544), (448, 448), (576, 576), (576, 576))
+HEAD_SPLITS = ((544, 544), (512, 512), (576, 576), (576, 576))
 PE_POS = 256
 V_POS = 128
-G_POS = 384
+G_POS = 416
 
 FLOPS = 2 * IMGS * 2 * P * 1024 * POS
 
@@ -52,7 +52,6 @@ def tile_fr_pa_t_kernel(tc, x1, x2, c1_w, c1_b, c2_w, c2_b, out_0, out_1):
         ident_b = const.tile([P, P], BF16, name="ident_b")
         w_sb = const.tile([P, 2, 1024], BF16, name="w_sb")
         b_rows = const.tile([P, P], BF16, name="b_rows")
-        b_f32 = const.tile([P, P], F32, name="b_f32")
         bias = const.tile([P, 2], F32, name="bias")
         res = const.tile([P, P], F32, name="res")
         warm = const.tile([P, 1], F32, name="warm")
@@ -114,8 +113,7 @@ def tile_fr_pa_t_kernel(tc, x1, x2, c1_w, c1_b, c2_w, c2_b, out_0, out_1):
         def regroup_sg(k):
             if not 0 <= k < TILES:
                 return
-            grp = grpp.tile([P, POS, PACK], BF16, name="grp", align_bytes=64)
-            grps[k] = grp
+            grp = grps[k]
             first, lo, hi = split_of(k)
             dst, src = views(k, hi, POS)
             nc.scalar.copy(out=dst, in_=src)
@@ -130,10 +128,11 @@ def tile_fr_pa_t_kernel(tc, x1, x2, c1_w, c1_b, c2_w, c2_b, out_0, out_1):
         def regroup_v(k):
             if not 0 <= k < TILES:
                 return
+            grp = grpp.tile([P, POS, PACK], BF16, name="grp", align_bytes=64)
+            grps[k] = grp
             first, lo, hi = split_of(k)
             dst, src = views(k, first, lo)
             nc.vector.tensor_copy(out=dst, in_=src)
-            load(k + RAW_BUFS)
 
         def quantise(k):
             if not 0 <= k < TILES:
@@ -214,10 +213,11 @@ def tile_fr_pa_t_kernel(tc, x1, x2, c1_w, c1_b, c2_w, c2_b, out_0, out_1):
             for g in range(2):
                 for u in range(2):
                     nc.tensor.transpose(wt[:, g, u, :], words[:, g, u, :], ident[:])
-            nc.vector.tensor_copy(
-                out=w_grp[:, i, :].bitcast(F32).rearrange("p (g o u) -> p g o u", g=2, u=2),
-                in_=wt[:].rearrange("p g u o -> p g o u"),
-            )
+            dst = w_grp[:, i, :].bitcast(F32).rearrange("p (g o u) -> p g o u", g=2, u=2)
+            if i == 0:
+                nc.vector.tensor_copy(out=dst, in_=wt[:].rearrange("p g u o -> p g o u"))
+            else:
+                nc.scalar.copy(out=dst, in_=wt[:].rearrange("p g u o -> p g o u"))
 
         def weight_quantise(i):
             wc = slice(i * 2 * P, (i + 1) * 2 * P)
@@ -225,15 +225,14 @@ def tile_fr_pa_t_kernel(tc, x1, x2, c1_w, c1_b, c2_w, c2_b, out_0, out_1):
 
         def weights_first():
             weight(0)
+            weight(1)
+            bt = psaux.tile([P, P], BF16, name="bt", tag="aux")
+            nc.tensor.transpose(bt[:], b_rows[:], ident_b[:])
+            nc.scalar.copy(out=bias[:], in_=bt[:, 0:2])
 
         def weights_rest():
             weight_quantise(0)
-            weight(1)
-            nc.vector.tensor_copy(out=b_f32[:], in_=b_rows[:])
-            bt = psaux.tile([P, P], F32, name="bt", tag="aux")
-            nc.tensor.transpose(bt[:], b_f32[:], ident[:])
             weight_quantise(1)
-            nc.vector.tensor_copy(out=bias[:], in_=bt[:, 0:2])
 
         make_identity(nc, ident[:])
         make_identity(nc, ident_b[:])
@@ -243,21 +242,24 @@ def tile_fr_pa_t_kernel(tc, x1, x2, c1_w, c1_b, c2_w, c2_b, out_0, out_1):
         nc.vector.memset(res[:], 0.0)
         load(0)
         nc.sync.dma_start(out=w_sb[:, 0, :], in_=c1_w)
-        load(1)
         nc.sync.dma_start(out=w_sb[:, 1, :], in_=c2_w)
         nc.sync.dma_start(out=b_rows[0:1, :], in_=c1_b.unsqueeze(0))
         nc.sync.dma_start(out=b_rows[1:2, :], in_=c2_b.unsqueeze(0))
-        for k in range(2, RAW_BUFS):
+        for k in range(1, RAW_BUFS):
             load(k)
 
         for u in range(-4, UNITS):
             spread(u + 5)
             exp_of_y(u + 1)
+            if u >= 0:
+                regroup_v(u + 4)
             quantise(u + 3)
             project(u + 2)
+            if u < 0:
+                regroup_v(u + 4)
             exp_of_a(u)
             regroup_sg(u + 4)
-            regroup_v(u + 4)
+            load(u + 4 + RAW_BUFS)
             if u == -4:
                 weights_first()
             if u == -3:

@@ -24,7 +24,7 @@ RAW_BUFS = 8
 HEAD_SPLITS = ((544, 544), (512, 512), (576, 576), (576, 576))
 PE_POS = 256
 V_POS = 128
-G_POS = 416
+G_POS = 384
 
 FLOPS = 2 * IMGS * 2 * P * 1024 * POS
 
@@ -251,12 +251,9 @@ def tile_fr_pa_t_kernel(tc, x1, x2, c1_w, c1_b, c2_w, c2_b, out_0, out_1):
         for u in range(-4, UNITS):
             spread(u + 5)
             exp_of_y(u + 1)
-            if u >= 0:
-                regroup_v(u + 4)
             quantise(u + 3)
             project(u + 2)
-            if u < 0:
-                regroup_v(u + 4)
+            regroup_v(u + 4)
             exp_of_a(u)
             regroup_sg(u + 4)
             load(u + 4 + RAW_BUFS)

@@ -23,8 +23,8 @@ RUN = 4
 RAW_BUFS = 8
 HEAD_SPLITS = ((544, 544), (512, 512), (576, 576), (576, 576))
 PE_POS = 256
-V_POS = 128
-G_POS = 384
+V_POS = 96
+G_POS = 416
 
 FLOPS = 2 * IMGS * 2 * P * 1024 * POS
 

@@ -24,7 +24,7 @@ RAW_BUFS = 8
 HEAD_SPLITS = ((544, 544), (512, 512), (576, 576), (576, 576))
 PE_POS = 256
 V_POS = 96
-G_POS = 416
+G_POS = 432
 
 FLOPS = 2 * IMGS * 2 * P * 1024 * POS
 

@@ -144,26 +144,26 @@ def tile_fr_pa_t_kernel(tc, x1, x2, c1_w, c1_b, c2_w, c2_b, out_0, out_1):
                 out=cod[:].bitcast(FP8X4), scales=scl[:], in_=grps[k][:].rearrange("p w t -> p (w t)")
             )
 
-        def project(u):
+        def project(u, g):
             if not 0 <= u < UNITS:
                 return
             n, i = u // 2, u % 2
             for h in range(2):
-                y = psum.tile([P, HALF], F32, name="y", tag="bank")
-                ys[(u, h)] = y
-                for g in range(2):
-                    wc = slice((i * 2 + g) * P, (i * 2 + g + 1) * P)
-                    xc = slice(h * HALF, (h + 1) * HALF)
-                    cod, scl = cods[2 * n + g]
-                    nc.tensor.matmul_mx(
-                        out=y[:],
-                        lhsT=w_cod[:, wc].bitcast(FP8X4),
-                        lhsT_scale=w_scl[:, wc],
-                        rhs=cod[:, xc].bitcast(FP8X4),
-                        rhs_scale=scl[:, xc],
-                        start=(g == 0),
-                        stop=(g == 1),
-                    )
+                if g == 0:
+                    y = psum.tile([P, HALF], F32, name="y", tag="bank")
+                    ys[(u, h)] = y
+                wc = slice((i * 2 + g) * P, (i * 2 + g + 1) * P)
+                xc = slice(h * HALF, (h + 1) * HALF)
+                cod, scl = cods[2 * n + g]
+                nc.tensor.matmul_mx(
+                    out=ys[(u, h)][:],
+                    lhsT=w_cod[:, wc].bitcast(FP8X4),
+                    lhsT_scale=w_scl[:, wc],
+                    rhs=cod[:, xc].bitcast(FP8X4),
+                    rhs_scale=scl[:, xc],
+                    start=(g == 0),
+                    stop=(g == 1),
+                )
 
         def exp_of_y(u):
             if not 0 <= u < UNITS:
@@ -251,8 +251,9 @@ def tile_fr_pa_t_kernel(tc, x1, x2, c1_w, c1_b, c2_w, c2_b, out_0, out_1):
         for u in range(-4, UNITS):
             spread(u + 5)
             exp_of_y(u + 1)
+            project(u + 2, 0)
             quantise(u + 3)
-            project(u + 2)
+            project(u + 2, 1)
             regroup_v(u + 4)
             exp_of_a(u)
             regroup_sg(u + 4)

@@ -23,8 +23,8 @@ RUN = 4
 RAW_BUFS = 8
 HEAD_SPLITS = ((544, 544), (512, 512), (576, 576), (576, 576))
 PE_POS = 256
-V_POS = 96
-G_POS = 432
+V_POS = 80
+G_POS = 496
 
 FLOPS = 2 * IMGS * 2 * P * 1024 * POS
 
@@ -118,12 +118,15 @@ def tile_fr_pa_t_kernel(tc, x1, x2, c1_w, c1_b, c2_w, c2_b, out_0, out_1):
             dst, src = views(k, hi, POS)
             nc.scalar.copy(out=dst, in_=src)
             if hi > lo:
+                dst, src = views(k, lo, hi)
                 nc.gpsimd.tensor_scalar(
-                    out=grp[:, lo:hi, :], in0=raws[k][:, :, lo:hi].rearrange("p t w -> p w t"),
-                    scalar1=1.0, scalar2=0.0, op0=ALU.mult, op1=ALU.add,
+                    out=dst, in0=src, scalar1=1.0, scalar2=0.0, op0=ALU.mult, op1=ALU.add,
                 )
             if through_pe(k):
-                nc.scalar.copy(out=grp[:, 0:PE_POS, :], in_=banks[k][:])
+                nc.scalar.copy(
+                    out=grp[:, 0:PE_POS, :].rearrange("p w t -> p (w t)").bitcast(F32),
+                    in_=banks[k][:].rearrange("p w t -> p (w t)").bitcast(F32),
+                )
 
         def regroup_v(k):
             if not 0 <= k < TILES:

@@ -21,18 +21,18 @@ POS = 1024
 HALF = 512
 RUN = 4
 RAW_BUFS = 8
-HEAD_SPLITS = ((544, 544), (512, 512), (576, 576), (576, 576))
-PE_POS = 256
-V_POS = 80
-G_POS = 496
+HEAD_SHARES = ((0, 640, 0), (0, 640, 0), (0, 576, 0), (128, 480, 0), (256, 72, 504))
+SHARES = (256, 72, 504)
+HEAD_PARTS = {0: (("v", 0, 640), ("s", 640, 1024))}
+FIRST_GATED = 99
+GATE = 0
 
 FLOPS = 2 * IMGS * 2 * P * 1024 * POS
 
 
-def split_of(k):
-    if k < len(HEAD_SPLITS):
-        return (0,) + HEAD_SPLITS[k]
-    return (PE_POS, PE_POS + V_POS, PE_POS + V_POS + G_POS)
+def bounds(k):
+    pe, v, g = HEAD_SHARES[k] if k < len(HEAD_SHARES) else SHARES
+    return pe, pe + v, pe + v + g
 
 
 def tile_fr_pa_t_kernel(tc, x1, x2, c1_w, c1_b, c2_w, c2_b, out_0, out_1):
@@ -80,62 +80,95 @@ def tile_fr_pa_t_kernel(tc, x1, x2, c1_w, c1_b, c2_w, c2_b, out_0, out_1):
             if not 0 <= k < TILES:
                 return
             src = (x1, x2)[k % 2][k // 2].rearrange("(p t) h w -> p t (h w)", t=PACK)
-            raw = rawp.tile([P, PACK, POS], BF16, name="raw")
-            raws[k] = raw
-            if k == 0:
-                cut = split_of(0)[1]
-                nc.sync.dma_start(out=raw[:, :, 0:cut], in_=src[:, :, 0:cut])
-                nc.sync.dma_start(out=raw[:, :, cut:POS], in_=src[:, :, cut:POS])
-            else:
-                nc.sync.dma_start(out=raw[:], in_=src)
+            cuts = {0: (0, 640, POS)}.get(k, (0, POS))
+            raws[k] = []
+            for j in range(len(cuts) - 1):
+                lo, hi = cuts[j], cuts[j + 1]
+                if lo == 0 and hi == POS:
+                    raw = rawp.tile([P, PACK, POS], BF16, name="raw")
+                else:
+                    raw = const.tile([P, PACK, hi - lo], BF16, name="raw%d_%d" % (k, j))
+                raws[k].append((raw, lo, hi))
+                nc.sync.dma_start(out=raw[:], in_=src[:, :, lo:hi])
 
-        def through_pe(k):
-            return k >= len(HEAD_SPLITS)
+        def raw_of(k, lo, hi):
+            for raw, a, b in raws[k]:
+                if a <= lo and hi <= b:
+                    return raw[:, :, lo - a : hi - a]
+            raise ValueError("no piece")
 
         def views(k, lo, hi):
             return (
                 grps[k][:, lo:hi, :].rearrange("p (c r) t -> p c t r", r=RUN),
-                raws[k][:, :, lo:hi].rearrange("p t (c r) -> p c t r", r=RUN),
+                raw_of(k, lo, hi).rearrange("p t (c r) -> p c t r", r=RUN),
             )
 
+        def new_grp(k):
+            if 0 <= k < TILES:
+                grps[k] = grpp.tile([P, POS, PACK], BF16, name="grp", align_bytes=64)
+
         def spread(k):
-            if not 0 <= k < TILES or not through_pe(k):
+            if not 0 <= k < TILES or bounds(k)[0] == 0:
                 return
-            bank = psaux.tile([P, PE_POS, PACK], BF16, name="bank", tag="aux")
+            pe = bounds(k)[0]
+            bank = psaux.tile([P, 2 * P, PACK], BF16, name="bank", tag="aux")
             banks[k] = bank
-            for c in range(PE_POS // P):
-                w = slice(c * P, (c + 1) * P)
+            for c in range(pe // P):
                 nc.tensor.matmul(
-                    out=bank[:, w, :], lhsT=ident_b[:], rhs=raws[k][:, :, w].rearrange("p t w -> p w t"),
+                    out=bank[:, c * P : (c + 1) * P, :], lhsT=ident_b[:],
+                    rhs=raw_of(k, c * P, (c + 1) * P).rearrange("p t w -> p w t"),
                     start=True, stop=True,
                 )
 
-        def regroup_sg(k):
+        def regroup_parts(k, engine):
+            for who, lo, hi in HEAD_PARTS[k]:
+                if who == engine:
+                    dst, src = views(k, lo, hi)
+                    if who == "v":
+                        nc.vector.tensor_copy(out=dst, in_=src)
+                    else:
+                        nc.scalar.copy(out=dst, in_=src)
+
+        def regroup_g(k):
             if not 0 <= k < TILES:
                 return
-            grp = grps[k]
-            first, lo, hi = split_of(k)
-            dst, src = views(k, hi, POS)
-            nc.scalar.copy(out=dst, in_=src)
+            pe, lo, hi = bounds(k)
             if hi > lo:
+                lo = max(pe, lo - GATE)
                 dst, src = views(k, lo, hi)
                 nc.gpsimd.tensor_scalar(
                     out=dst, in0=src, scalar1=1.0, scalar2=0.0, op0=ALU.mult, op1=ALU.add,
                 )
-            if through_pe(k):
-                nc.scalar.copy(
-                    out=grp[:, 0:PE_POS, :].rearrange("p w t -> p (w t)").bitcast(F32),
-                    in_=banks[k][:].rearrange("p w t -> p (w t)").bitcast(F32),
-                )
+
+        def regroup_s(k):
+            if not 0 <= k < TILES:
+                return
+            if k in HEAD_PARTS:
+                regroup_parts(k, "s")
+                return
+            pe, lo, hi = bounds(k)
+            dst, src = views(k, hi, POS)
+            nc.scalar.copy(out=dst, in_=src)
+
+        def bank_s(k):
+            if not 0 <= k < TILES or bounds(k)[0] == 0:
+                return
+            pe = bounds(k)[0]
+            nc.scalar.copy(
+                out=grps[k][:, 0:pe, :].rearrange("p w t -> p (w t)").bitcast(F32),
+                in_=banks[k][:, 0:pe, :].rearrange("p w t -> p (w t)").bitcast(F32),
+            )
 
         def regroup_v(k):
             if not 0 <= k < TILES:
                 return
-            grp = grpp.tile([P, POS, PACK], BF16, name="grp", align_bytes=64)
-            grps[k] = grp
-            first, lo, hi = split_of(k)
-            dst, src = views(k, first, lo)
-            nc.vector.tensor_copy(out=dst, in_=src)
+            if k in HEAD_PARTS:
+                regroup_parts(k, "v")
+                return
+            pe, lo, hi = bounds(k)
+            if lo > pe:
+                dst, src = views(k, pe, lo)
+                nc.vector.tensor_copy(out=dst, in_=src)
 
         def quantise(k):
             if not 0 <= k < TILES:
@@ -153,7 +186,10 @@ def tile_fr_pa_t_kernel(tc, x1, x2, c1_w, c1_b, c2_w, c2_b, out_0, out_1):
             n, i = u // 2, u % 2
             for h in range(2):
                 if g == 0:
-                    y = psum.tile([P, HALF], F32, name="y", tag="bank")
+                    if u == UNITS - 1:
+                        y = psaux.tile([P, HALF], F32, name="y_last", tag="aux")
+                    else:
+                        y = psum.tile([P, HALF], F32, name="y", tag="bank")
                     ys[(u, h)] = y
                 wc = slice((i * 2 + g) * P, (i * 2 + g + 1) * P)
                 xc = slice(h * HALF, (h + 1) * HALF)
@@ -197,16 +233,20 @@ def tile_fr_pa_t_kernel(tc, x1, x2, c1_w, c1_b, c2_w, c2_b, out_0, out_1):
                 accum_out=sum_e[:, col : col + 1],
             )
 
-        def weigh(u):
+        def weigh(u, gated):
             if not 0 <= u < UNITS:
                 return
             col = column_of(u)
             if u == UNITS - 1:
                 nc.vector.reciprocal(out=rec[:], in_=sum_e[:])
-            for h in range(2):
+            for h in (1, 0):
                 half = exps[u][:, h * HALF : (h + 1) * HALF]
+                out = half
+                if h == 1 and FIRST_GATED <= gated < TILES:
+                    lo = bounds(gated)[1]
+                    out = grps[gated][:, lo : lo + 2 * P, :].rearrange("p w t -> p (w t)").bitcast(F32)
                 nc.vector.scalar_tensor_tensor(
-                    out=half, in0=ys[(u, h)][:], scalar=bias[:, u % 2 : u % 2 + 1], in1=half,
+                    out=out, in0=ys[(u, h)][:], scalar=bias[:, u % 2 : u % 2 + 1], in1=half,
                     op0=ALU.add, op1=ALU.mult, accum_out=sum_ey[:, col, h : h + 1],
                 )
 
@@ -217,14 +257,7 @@ def tile_fr_pa_t_kernel(tc, x1, x2, c1_w, c1_b, c2_w, c2_b, out_0, out_1):
                 for u in range(2):
                     nc.tensor.transpose(wt[:, g, u, :], words[:, g, u, :], ident[:])
             dst = w_grp[:, i, :].bitcast(F32).rearrange("p (g o u) -> p g o u", g=2, u=2)
-            if i == 0:
-                nc.vector.tensor_copy(out=dst, in_=wt[:].rearrange("p g u o -> p g o u"))
-            else:
-                nc.scalar.copy(out=dst, in_=wt[:].rearrange("p g u o -> p g o u"))
-
-        def weight_quantise(i):
-            wc = slice(i * 2 * P, (i + 1) * 2 * P)
-            nc.vector.quantize_mx(out=w_cod[:, wc].bitcast(FP8X4), scales=w_scl[:, wc], in_=w_grp[:, i, :])
+            nc.scalar.copy(out=dst, in_=wt[:].rearrange("p g u o -> p g o u"))
 
         def weights_first():
             weight(0)
@@ -234,8 +267,9 @@ def tile_fr_pa_t_kernel(tc, x1, x2, c1_w, c1_b, c2_w, c2_b, out_0, out_1):
             nc.scalar.copy(out=bias[:], in_=bt[:, 0:2])
 
         def weights_rest():
-            weight_quantise(0)
-            weight_quantise(1)
+            nc.vector.quantize_mx(
+                out=w_cod[:].bitcast(FP8X4), scales=w_scl[:], in_=w_grp[:].rearrange("p i c -> p (i c)")
+            )
 
         make_identity(nc, ident[:])
         make_identity(nc, ident_b[:])
@@ -252,21 +286,29 @@ def tile_fr_pa_t_kernel(tc, x1, x2, c1_w, c1_b, c2_w, c2_b, out_0, out_1):
             load(k)
 
         for u in range(-4, UNITS):
-            spread(u + 5)
             exp_of_y(u + 1)
             project(u + 2, 0)
+            if u >= 0:
+                spread(u + 5)
+            if u == -4:
+                new_grp(0)
             quantise(u + 3)
             project(u + 2, 1)
+            if u < 0:
+                spread(u + 5)
             regroup_v(u + 4)
             exp_of_a(u)
-            regroup_sg(u + 4)
+            regroup_s(u + 4)
+            regroup_g(u + 4)
+            bank_s(u + 4)
             load(u + 4 + RAW_BUFS)
             if u == -4:
                 weights_first()
             if u == -3:
                 weights_rest()
+            new_grp(u + 5)
             peak(u + 1)
-            weigh(u)
+            weigh(u, u + 5)
 
         nc.vector.tensor_tensor(out=num[:], in0=sum_ey[:, :, 0], in1=sum_ey[:, :, 1], op=ALU.add)
         nc.vector.tensor_tensor(out=res[:, 0:UNITS], in0=num[:], in1=rec[:], op=ALU.mult)

@@ -17,13 +17,14 @@ PACK = 4
 IMGS = 8
 TILES = 2 * IMGS
 UNITS = 2 * IMGS
+COLS = UNITS + 1
 POS = 1024
 HALF = 512
 RUN = 4
 RAW_BUFS = 8
-HEAD_SHARES = ((0, 640, 0), (0, 640, 0), (0, 576, 0), (128, 480, 0), (256, 72, 504))
+HEAD_SHARES = ((0, 640, 128), (0, 640, 0), (0, 576, 0), (128, 480, 0))
 SHARES = (256, 72, 504)
-HEAD_PARTS = {0: (("v", 0, 640), ("s", 640, 1024))}
+HEAD_PARTS = {0: (("v", 0, 640), ("s", 768, 1024))}
 FIRST_GATED = 99
 GATE = 0
 
@@ -58,10 +59,10 @@ def tile_fr_pa_t_kernel(tc, x1, x2, c1_w, c1_b, c2_w, c2_b, out_0, out_1):
         w_grp = const.tile([P, 2, 2 * P * PACK], BF16, name="w_grp", align_bytes=64)
         w_cod = const.tile([P, 2 * 2 * P], U32, name="w_cod", align_bytes=64)
         w_scl = const.tile([P, 2 * 2 * P], U8, name="w_scl", align_bytes=64)
-        sum_e = const.tile([P, UNITS], F32, name="sum_e")
-        sum_ey = const.tile([P, UNITS, 2], F32, name="sum_ey")
-        num = const.tile([P, UNITS], F32, name="num")
-        rec = const.tile([P, UNITS], F32, name="rec")
+        sum_e = const.tile([P, COLS], F32, name="sum_e")
+        sum_ey = const.tile([P, COLS, 2], F32, name="sum_ey")
+        num = const.tile([P, COLS], F32, name="num")
+        rec = const.tile([P, COLS], F32, name="rec")
         rows = const.tile([P, P], F32, name="rows")
 
         raws = {}
@@ -74,7 +75,7 @@ def tile_fr_pa_t_kernel(tc, x1, x2, c1_w, c1_b, c2_w, c2_b, out_0, out_1):
         banks = {}
 
         def column_of(u):
-            return (u % 2) * IMGS + u // 2
+            return (u % 2) * (IMGS + 1) + u // 2
 
         def load(k):
             if not 0 <= k < TILES:
@@ -238,7 +239,13 @@ def tile_fr_pa_t_kernel(tc, x1, x2, c1_w, c1_b, c2_w, c2_b, out_0, out_1):
                 return
             col = column_of(u)
             if u == UNITS - 1:
+                nc.gpsimd.tensor_tensor(
+                    out=num[:, 0 : COLS - 1], in0=sum_ey[:, 0 : COLS - 1, 0], in1=sum_ey[:, 0 : COLS - 1, 1], op=ALU.add
+                )
                 nc.vector.reciprocal(out=rec[:], in_=sum_e[:])
+                nc.gpsimd.tensor_tensor(
+                    out=res[:, 0 : COLS - 1], in0=num[:, 0 : COLS - 1], in1=rec[:, 0 : COLS - 1], op=ALU.mult
+                )
             for h in (1, 0):
                 half = exps[u][:, h * HALF : (h + 1) * HALF]
                 out = half
@@ -259,17 +266,14 @@ def tile_fr_pa_t_kernel(tc, x1, x2, c1_w, c1_b, c2_w, c2_b, out_0, out_1):
             dst = w_grp[:, i, :].bitcast(F32).rearrange("p (g o u) -> p g o u", g=2, u=2)
             nc.scalar.copy(out=dst, in_=wt[:].rearrange("p g u o -> p g o u"))
 
-        def weights_first():
-            weight(0)
-            weight(1)
+        def weight_quantise(i):
+            wc = slice(i * 2 * P, (i + 1) * 2 * P)
+            nc.vector.quantize_mx(out=w_cod[:, wc].bitcast(FP8X4), scales=w_scl[:, wc], in_=w_grp[:, i, :])
+
+        def biases():
             bt = psaux.tile([P, P], BF16, name="bt", tag="aux")
             nc.tensor.transpose(bt[:], b_rows[:], ident_b[:])
             nc.scalar.copy(out=bias[:], in_=bt[:, 0:2])
-
-        def weights_rest():
-            nc.vector.quantize_mx(
-                out=w_cod[:].bitcast(FP8X4), scales=w_scl[:], in_=w_grp[:].rearrange("p i c -> p (i c)")
-            )
 
         make_identity(nc, ident[:])
         make_identity(nc, ident_b[:])
@@ -277,12 +281,15 @@ def tile_fr_pa_t_kernel(tc, x1, x2, c1_w, c1_b, c2_w, c2_b, out_0, out_1):
         nc.scalar.activation(out=warm[:], in_=warm[:], func=ACT.Exp)
         nc.vector.memset(b_rows[:], 0.0)
         nc.vector.memset(res[:], 0.0)
+        nc.vector.memset(sum_e[:], 1.0)
+        nc.vector.memset(sum_ey[:], 0.0)
         load(0)
         nc.sync.dma_start(out=w_sb[:, 0, :], in_=c1_w)
-        nc.sync.dma_start(out=w_sb[:, 1, :], in_=c2_w)
         nc.sync.dma_start(out=b_rows[0:1, :], in_=c1_b.unsqueeze(0))
         nc.sync.dma_start(out=b_rows[1:2, :], in_=c2_b.unsqueeze(0))
-        for k in range(1, RAW_BUFS):
+        load(1)
+        nc.sync.dma_start(out=w_sb[:, 1, :], in_=c2_w)
+        for k in range(2, RAW_BUFS):
             load(k)
 
         for u in range(-4, UNITS):
@@ -293,6 +300,8 @@ def tile_fr_pa_t_kernel(tc, x1, x2, c1_w, c1_b, c2_w, c2_b, out_0, out_1):
             if u == -4:
                 new_grp(0)
             quantise(u + 3)
+            if u == -3:
+                weight_quantise(0)
             project(u + 2, 1)
             if u < 0:
                 spread(u + 5)
@@ -303,17 +312,23 @@ def tile_fr_pa_t_kernel(tc, x1, x2, c1_w, c1_b, c2_w, c2_b, out_0, out_1):
             bank_s(u + 4)
             load(u + 4 + RAW_BUFS)
             if u == -4:
-                weights_first()
+                weight(0)
+                biases()
             if u == -3:
-                weights_rest()
+                weight(1)
+            if u == -2:
+                weight_quantise(1)
             new_grp(u + 5)
             peak(u + 1)
             weigh(u, u + 5)
 
-        nc.vector.tensor_tensor(out=num[:], in0=sum_ey[:, :, 0], in1=sum_ey[:, :, 1], op=ALU.add)
-        nc.vector.tensor_tensor(out=res[:, 0:UNITS], in0=num[:], in1=rec[:], op=ALU.mult)
+        last = slice(COLS - 1, COLS)
+        nc.vector.tensor_scalar(
+            out=res[:, last], in0=sum_ey[:, last, 0], scalar1=sum_ey[:, COLS - 1, 1:2], scalar2=rec[:, last],
+            op0=ALU.add, op1=ALU.mult,
+        )
         rt = psaux.tile([P, P], F32, name="rt", tag="aux")
         nc.tensor.transpose(rt[:], res[:], ident[:])
         nc.vector.tensor_copy(out=rows[:], in_=rt[:])
-        nc.sync.dma_start(out=out_0, in_=rows[0:IMGS, :])
-        nc.sync.dma_start(out=out_1, in_=rows[IMGS : 2 * IMGS, :])
+        nc.scalar.dma_start(out=out_0, in_=rows[0:IMGS, :])
+        nc.sync.dma_start(out=out_1, in_=rows[IMGS + 1 : COLS, :])

@@ -22,8 +22,8 @@ POS = 1024
 HALF = 512
 RUN = 4
 RAW_BUFS = 8
-HEAD_SHARES = ((0, 640, 128), (0, 640, 0), (0, 576, 0), (128, 480, 0))
-SHARES = (256, 72, 504)
+HEAD_SHARES = ((0, 640, 128), (0, 640, 0), (0, 576, 0), (128, 480, 0), (256, 240, 240))
+SHARES = (256, 64, 496)
 HEAD_PARTS = {0: (("v", 0, 640), ("s", 768, 1024))}
 FIRST_GATED = 99
 GATE = 0

@@ -98,10 +98,10 @@ def tile_fr_pa_t_kernel(tc, x1, x2, c1_w, c1_b, c2_w, c2_b, out_0, out_1):
                     return raw[:, :, lo - a : hi - a]
             raise ValueError("no piece")
 
-        def views(k, lo, hi):
+        def views(k, lo, hi, run=2 * RUN):
             return (
-                grps[k][:, lo:hi, :].rearrange("p (c r) t -> p c t r", r=RUN),
-                raw_of(k, lo, hi).rearrange("p t (c r) -> p c t r", r=RUN),
+                grps[k][:, lo:hi, :].rearrange("p (c r) t -> p c t r", r=run),
+                raw_of(k, lo, hi).rearrange("p t (c r) -> p c t r", r=run),
             )
 
         def new_grp(k):
@@ -124,7 +124,7 @@ def tile_fr_pa_t_kernel(tc, x1, x2, c1_w, c1_b, c2_w, c2_b, out_0, out_1):
         def regroup_parts(k, engine):
             for who, lo, hi in HEAD_PARTS[k]:
                 if who == engine:
-                    dst, src = views(k, lo, hi)
+                    dst, src = views(k, lo, hi, RUN if who == "v" else 2 * RUN)
                     if who == "v":
                         nc.vector.tensor_copy(out=dst, in_=src)
                     else:
@@ -168,7 +168,7 @@ def tile_fr_pa_t_kernel(tc, x1, x2, c1_w, c1_b, c2_w, c2_b, out_0, out_1):
                 return
             pe, lo, hi = bounds(k)
             if lo > pe:
-                dst, src = views(k, pe, lo)
+                dst, src = views(k, pe, lo, RUN)
                 nc.vector.tensor_copy(out=dst, in_=src)
 
         def quantise(k):

from contextlib import ExitStack

import concourse.mybir as mybir
from concourse.masks import make_identity

FP8X4 = mybir.dt.float8_e4m3fn_x4
BF16 = mybir.dt.bfloat16
F32 = mybir.dt.float32
U32 = mybir.dt.uint32
U8 = mybir.dt.uint8
ACT = mybir.ActivationFunctionType
ALU = mybir.AluOpType
AX = mybir.AxisListType

P = 128
PACK = 4
IMGS = 8
TILES = 2 * IMGS
UNITS = 2 * IMGS
COLS = UNITS + 1
POS = 1024
HALF = 512
RUN = 4
RAW_BUFS = 8
HEAD_SHARES = ((0, 640, 128), (0, 640, 0), (0, 576, 0), (128, 480, 0), (256, 240, 240))
SHARES = (256, 64, 496)
HEAD_PARTS = {0: (("v", 0, 640), ("s", 768, 1024))}
FIRST_GATED = 99
GATE = 0

FLOPS = 2 * IMGS * 2 * P * 1024 * POS


def bounds(k):
    pe, v, g = HEAD_SHARES[k] if k < len(HEAD_SHARES) else SHARES
    return pe, pe + v, pe + v + g


def tile_fr_pa_t_kernel(tc, x1, x2, c1_w, c1_b, c2_w, c2_b, out_0, out_1):
    nc = tc.nc
    with ExitStack() as ctx:
        ctx.enter_context(tc.manual_schedule())
        const = ctx.enter_context(tc.tile_pool(name="const", bufs=1))
        rawp = ctx.enter_context(tc.tile_pool(name="rawp", bufs=RAW_BUFS))
        grpp = ctx.enter_context(tc.tile_pool(name="grpp", bufs=2))
        codp = ctx.enter_context(tc.tile_pool(name="codp", bufs=4))
        work = ctx.enter_context(tc.tile_pool(name="work", bufs=3))
        small = ctx.enter_context(tc.tile_pool(name="small", bufs=4))
        psum = ctx.enter_context(tc.psum_pool(name="psum", bufs=6))
        psaux = ctx.enter_context(tc.psum_pool(name="psaux", bufs=2))

        ident = const.tile([P, P], F32, name="ident")
        ident_b = const.tile([P, P], BF16, name="ident_b")
        w_sb = const.tile([P, 2, 1024], BF16, name="w_sb")
        b_rows = const.tile([P, P], BF16, name="b_rows")
        bias = const.tile([P, 2], F32, name="bias")
        res = const.tile([P, P], F32, name="res")
        warm = const.tile([P, 1], F32, name="warm")
        w_grp = const.tile([P, 2, 2 * P * PACK], BF16, name="w_grp", align_bytes=64)
        w_cod = const.tile([P, 2 * 2 * P], U32, name="w_cod", align_bytes=64)
        w_scl = const.tile([P, 2 * 2 * P], U8, name="w_scl", align_bytes=64)
        sum_e = const.tile([P, COLS], F32, name="sum_e")
        sum_ey = const.tile([P, COLS, 2], F32, name="sum_ey")
        num = const.tile([P, COLS], F32, name="num")
        rec = const.tile([P, COLS], F32, name="rec")
        rows = const.tile([P, P], F32, name="rows")

        raws = {}
        grps = {}
        cods = {}
        ys = {}
        acts = {}
        peaks = {}
        exps = {}
        banks = {}

        def column_of(u):
            return (u % 2) * (IMGS + 1) + u // 2

        def load(k):
            if not 0 <= k < TILES:
                return
            src = (x1, x2)[k % 2][k // 2].rearrange("(p t) h w -> p t (h w)", t=PACK)
            cuts = {0: (0, 640, POS)}.get(k, (0, POS))
            raws[k] = []
            for j in range(len(cuts) - 1):
                lo, hi = cuts[j], cuts[j + 1]
                if lo == 0 and hi == POS:
                    raw = rawp.tile([P, PACK, POS], BF16, name="raw")
                else:
                    raw = const.tile([P, PACK, hi - lo], BF16, name="raw%d_%d" % (k, j))
                raws[k].append((raw, lo, hi))
                nc.sync.dma_start(out=raw[:], in_=src[:, :, lo:hi])

        def raw_of(k, lo, hi):
            for raw, a, b in raws[k]:
                if a <= lo and hi <= b:
                    return raw[:, :, lo - a : hi - a]
            raise ValueError("no piece")

        def views(k, lo, hi, run=2 * RUN):
            return (
                grps[k][:, lo:hi, :].rearrange("p (c r) t -> p c t r", r=run),
                raw_of(k, lo, hi).rearrange("p t (c r) -> p c t r", r=run),
            )

        def new_grp(k):
            if 0 <= k < TILES:
                grps[k] = grpp.tile([P, POS, PACK], BF16, name="grp", align_bytes=64)

        def spread(k):
            if not 0 <= k < TILES or bounds(k)[0] == 0:
                return
            pe = bounds(k)[0]
            bank = psaux.tile([P, 2 * P, PACK], BF16, name="bank", tag="aux")
            banks[k] = bank
            for c in range(pe // P):
                nc.tensor.matmul(
                    out=bank[:, c * P : (c + 1) * P, :], lhsT=ident_b[:],
                    rhs=raw_of(k, c * P, (c + 1) * P).rearrange("p t w -> p w t"),
                    start=True, stop=True,
                )

        def regroup_parts(k, engine):
            for who, lo, hi in HEAD_PARTS[k]:
                if who == engine:
                    dst, src = views(k, lo, hi, RUN if who == "v" else 2 * RUN)
                    if who == "v":
                        nc.vector.tensor_copy(out=dst, in_=src)
                    else:
                        nc.scalar.copy(out=dst, in_=src)

        def regroup_g(k):
            if not 0 <= k < TILES:
                return
            pe, lo, hi = bounds(k)
            if hi > lo:
                lo = max(pe, lo - GATE)
                dst, src = views(k, lo, hi)
                nc.gpsimd.tensor_scalar(
                    out=dst, in0=src, scalar1=1.0, scalar2=0.0, op0=ALU.mult, op1=ALU.add,
                )

        def regroup_s(k):
            if not 0 <= k < TILES:
                return
            if k in HEAD_PARTS:
                regroup_parts(k, "s")
                return
            pe, lo, hi = bounds(k)
            dst, src = views(k, hi, POS)
            nc.scalar.copy(out=dst, in_=src)

        def bank_s(k):
            if not 0 <= k < TILES or bounds(k)[0] == 0:
                return
            pe = bounds(k)[0]
            nc.scalar.copy(
                out=grps[k][:, 0:pe, :].rearrange("p w t -> p (w t)").bitcast(F32),
                in_=banks[k][:, 0:pe, :].rearrange("p w t -> p (w t)").bitcast(F32),
            )

        def regroup_v(k):
            if not 0 <= k < TILES:
                return
            if k in HEAD_PARTS:
                regroup_parts(k, "v")
                return
            pe, lo, hi = bounds(k)
            if lo > pe:
                dst, src = views(k, pe, lo, RUN)
                nc.vector.tensor_copy(out=dst, in_=src)

        def quantise(k):
            if not 0 <= k < TILES:
                return
            cod = codp.tile([P, POS], U32, name="cod", align_bytes=64)
            scl = codp.tile([P, POS], U8, name="scl", align_bytes=64)
            cods[k] = (cod, scl)
            nc.vector.quantize_mx(
                out=cod[:].bitcast(FP8X4), scales=scl[:], in_=grps[k][:].rearrange("p w t -> p (w t)")
            )

        def project(u, g):
            if not 0 <= u < UNITS:
                return
            n, i = u // 2, u % 2
            for h in range(2):
                if g == 0:
                    if u == UNITS - 1:
                        y = psaux.tile([P, HALF], F32, name="y_last", tag="aux")
                    else:
                        y = psum.tile([P, HALF], F32, name="y", tag="bank")
                    ys[(u, h)] = y
                wc = slice((i * 2 + g) * P, (i * 2 + g + 1) * P)
                xc = slice(h * HALF, (h + 1) * HALF)
                cod, scl = cods[2 * n + g]
                nc.tensor.matmul_mx(
                    out=ys[(u, h)][:],
                    lhsT=w_cod[:, wc].bitcast(FP8X4),
                    lhsT_scale=w_scl[:, wc],
                    rhs=cod[:, xc].bitcast(FP8X4),
                    rhs_scale=scl[:, xc],
                    start=(g == 0),
                    stop=(g == 1),
                )

        def exp_of_y(u):
            if not 0 <= u < UNITS:
                return
            a = work.tile([P, POS], F32, name="a")
            acts[u] = a
            for h in range(2):
                nc.scalar.activation(
                    out=a[:, h * HALF : (h + 1) * HALF], in_=ys[(u, h)][:], func=ACT.Exp,
                    bias=bias[:, u % 2 : u % 2 + 1], scale=1.0,
                )

        def peak(u):
            if not 0 <= u < UNITS:
                return
            negmax = small.tile([P, 1], F32, name="negmax")
            peaks[u] = negmax
            nc.vector.tensor_reduce(out=negmax[:], in_=acts[u][:], axis=AX.X, op=ALU.max, negate=True)

        def exp_of_a(u):
            if not 0 <= u < UNITS:
                return
            e = work.tile([P, POS], F32, name="e")
            exps[u] = e
            col = column_of(u)
            nc.scalar.activation(
                out=e[:], in_=acts[u][:], func=ACT.Exp, bias=peaks[u][:], scale=1.0,
                accum_out=sum_e[:, col : col + 1],
            )

        def weigh(u, gated):
            if not 0 <= u < UNITS:
                return
            col = column_of(u)
            if u == UNITS - 1:
                nc.gpsimd.tensor_tensor(
                    out=num[:, 0 : COLS - 1], in0=sum_ey[:, 0 : COLS - 1, 0], in1=sum_ey[:, 0 : COLS - 1, 1], op=ALU.add
                )
                nc.vector.reciprocal(out=rec[:], in_=sum_e[:])
                nc.gpsimd.tensor_tensor(
                    out=res[:, 0 : COLS - 1], in0=num[:, 0 : COLS - 1], in1=rec[:, 0 : COLS - 1], op=ALU.mult
                )
            for h in (1, 0):
                half = exps[u][:, h * HALF : (h + 1) * HALF]
                out = half
                if h == 1 and FIRST_GATED <= gated < TILES:
                    lo = bounds(gated)[1]
                    out = grps[gated][:, lo : lo + 2 * P, :].rearrange("p w t -> p (w t)").bitcast(F32)
                nc.vector.scalar_tensor_tensor(
                    out=out, in0=ys[(u, h)][:], scalar=bias[:, u % 2 : u % 2 + 1], in1=half,
                    op0=ALU.add, op1=ALU.mult, accum_out=sum_ey[:, col, h : h + 1],
                )

        def weight(i):
            wt = psaux.tile([P, 2, 2, P], F32, name="wt", tag="aux")
            words = w_sb[:, i, :].bitcast(F32).rearrange("o (g p u) -> o g u p", g=2, u=2)
            for g in range(2):
                for u in range(2):
                    nc.tensor.transpose(wt[:, g, u, :], words[:, g, u, :], ident[:])
            dst = w_grp[:, i, :].bitcast(F32).rearrange("p (g o u) -> p g o u", g=2, u=2)
            nc.scalar.copy(out=dst, in_=wt[:].rearrange("p g u o -> p g o u"))

        def weight_quantise(i):
            wc = slice(i * 2 * P, (i + 1) * 2 * P)
            nc.vector.quantize_mx(out=w_cod[:, wc].bitcast(FP8X4), scales=w_scl[:, wc], in_=w_grp[:, i, :])

        def biases():
            bt = psaux.tile([P, P], BF16, name="bt", tag="aux")
            nc.tensor.transpose(bt[:], b_rows[:], ident_b[:])
            nc.scalar.copy(out=bias[:], in_=bt[:, 0:2])

        make_identity(nc, ident[:])
        make_identity(nc, ident_b[:])
        nc.vector.memset(warm[:], 0.0)
        nc.scalar.activation(out=warm[:], in_=warm[:], func=ACT.Exp)
        nc.vector.memset(b_rows[:], 0.0)
        nc.vector.memset(res[:], 0.0)
        nc.vector.memset(sum_e[:], 1.0)
        nc.vector.memset(sum_ey[:], 0.0)
        load(0)
        nc.sync.dma_start(out=w_sb[:, 0, :], in_=c1_w)
        nc.sync.dma_start(out=b_rows[0:1, :], in_=c1_b.unsqueeze(0))
        nc.sync.dma_start(out=b_rows[1:2, :], in_=c2_b.unsqueeze(0))
        load(1)
        nc.sync.dma_start(out=w_sb[:, 1, :], in_=c2_w)
        for k in range(2, RAW_BUFS):
            load(k)

        for u in range(-4, UNITS):
            exp_of_y(u + 1)
            project(u + 2, 0)
            if u >= 0:
                spread(u + 5)
            if u == -4:
                new_grp(0)
            quantise(u + 3)
            if u == -3:
                weight_quantise(0)
            project(u + 2, 1)
            if u < 0:
                spread(u + 5)
            regroup_v(u + 4)
            exp_of_a(u)
            regroup_s(u + 4)
            regroup_g(u + 4)
            bank_s(u + 4)
            load(u + 4 + RAW_BUFS)
            if u == -4:
                weight(0)
                biases()
            if u == -3:
                weight(1)
            if u == -2:
                weight_quantise(1)
            new_grp(u + 5)
            peak(u + 1)
            weigh(u, u + 5)

        last = slice(COLS - 1, COLS)
        nc.vector.tensor_scalar(
            out=res[:, last], in0=sum_ey[:, last, 0], scalar1=sum_ey[:, COLS - 1, 1:2], scalar2=rec[:, last],
            op0=ALU.add, op1=ALU.mult,
        )
        rt = psaux.tile([P, P], F32, name="rt", tag="aux")
        nc.tensor.transpose(rt[:], res[:], ident[:])
        nc.vector.tensor_copy(out=rows[:], in_=rt[:])
        nc.scalar.dma_start(out=out_0, in_=rows[0:IMGS, :])
        nc.sync.dma_start(out=out_1, in_=rows[IMGS + 1 : COLS, :])
